import numpy as np
import ml_dtypes


def mxq(x, axis, fmt="e4m3"):
    dtype, down = {"e4m3": (ml_dtypes.float8_e4m3fn, 7), "e5m2": (ml_dtypes.float8_e5m2, 14)}[fmt]
    v = np.moveaxis(np.asarray(x, np.float32).astype(ml_dtypes.bfloat16).astype(np.float64), axis, -1)
    blocks = v.reshape(v.shape[:-1] + (-1, 32))
    amax = np.abs(blocks).max(-1, keepdims=True)
    byte = np.maximum(np.where(amax > 0, np.frexp(amax)[1] - 1 + 127, 0) - down, 1)
    scale = np.exp2(byte - 127.0)
    codes = (blocks / scale).astype(np.float32).astype(dtype).astype(np.float64)
    return np.moveaxis((codes * scale).reshape(v.shape), -1, axis)


WIDE = False


def mx_kscale(k):
    if not WIDE:
        return np.ones(k)
    levels = np.array([30, -30])
    if k % 512:
        return np.exp2(np.random.permutation(np.resize(levels, k // 32))).repeat(32)
    a = np.empty((k // 512, 16))
    for p in range(k // 512):
        a[p, :8] = np.random.permutation(np.resize(levels, 8))
        for g in range(8):
            far = levels[np.abs(levels - a[p, g]) >= 10]
            a[p, g + 8] = far[np.random.randint(len(far))]
    return np.exp2(a.ravel()).repeat(32)


BF16 = ml_dtypes.bfloat16


def bf(x):
    return np.asarray(x, np.float32).astype(BF16)


def f64(x):
    return np.asarray(x).astype(np.float64)


B, SIDE, HE, Z, HD, XO = 1024, 32, 1024, 512, 2048, 1024


def setup_inputs():
    n = np.random.standard_normal
    s = mx_kscale(HD)
    return {"hd": bf(np.tanh(n((B, HD))) * s),
            "W_mu_d": bf(n((XO, HD)) * 1.5 / np.sqrt(HD) / s[None, :]),
            "b_mu_d": bf(n(XO) * 0.3),
            "W_ls_d": bf(n((XO, HD)) * 1.5 / np.sqrt(HD) / s[None, :]),
            "b_ls_d": bf(n(XO) * 0.3),
            "eps_x": bf(n((B, XO)))}


def reference(hd, W_mu_d, b_mu_d, W_ls_d, b_ls_d, eps_x):
    hq = mxq(f64(hd), 1, "e5m2")
    mu_d = (hq @ mxq(f64(W_mu_d), 1, "e4m3").T) + f64(b_mu_d)
    ls_d = (hq @ mxq(f64(W_ls_d), 1, "e4m3").T) + f64(b_ls_d)
    return mu_d + np.exp(0.5 * ls_d) * f64(eps_x)

@@ -1,0 +1,245 @@
+from contextlib import ExitStack
+
+import concourse.mybir as mybir
+from concourse.masks import make_identity
+
+B, K, XO = 1024, 2048, 1024
+FLOPS = 2 * 2 * B * K * XO
+
+F32 = mybir.dt.float32
+BF16 = mybir.dt.bfloat16
+U32 = mybir.dt.uint32
+U8 = mybir.dt.uint8
+E5M2X4 = mybir.dt.float8_e5m2_x4
+E4M3X4 = mybir.dt.float8_e4m3fn_x4
+ADD = mybir.AluOpType.add
+MULT = mybir.AluOpType.mult
+EXP = mybir.ActivationFunctionType.Exp
+
+P = 128
+K_PASS = 512
+PASSES = K // K_PASS
+WORDS = K_PASS // 2
+STRIP = 512
+TILES = STRIP // P
+COLS = STRIP // 2
+
+SORTER = [""] + ["vector"] * 8 + ["scalar"] * 3
+SORTER2 = [""] + ["vector"] * 4 + [""] * 4 + ["scalar"] * 3
+WHOLE = {8: 2, 9: 4, 10: 4, 11: 10}
+OUT_BUFS = 18
+SPT = 1
+FOLD = 16
+
+
+def tile_vae_pb_kernel(tc, hd, W_mu_d, b_mu_d, W_ls_d, b_ls_d, eps_x, out):
+    nc = tc.nc
+
+    runs = [[("w0", g), ("h0", g)] for g in range(PASSES)]
+    for strip in ("w1", "h1", "w2", "w3"):
+        runs.extend([[(strip, 0), (strip, 1)], [(strip, 2), (strip, 3)]])
+
+    matmuls = [[] for r in runs]
+    for g in range(PASSES):
+        matmuls[g + 1] = [(m, 0, g) for m in range(TILES)]
+    for first, rows, q in ((5, range(TILES), 1), (7, range(TILES, 2 * TILES), 0)):
+        for half in range(2):
+            matmuls[first + half] = [(m, q, g) for m in rows for g in (2 * half, 2 * half + 1)]
+    rest = [(m, 1) for m in range(TILES, 2 * TILES)] + [(m, q) for q in (2, 3) for m in range(2 * TILES)]
+    for r in sorted(WHOLE):
+        matmuls[r] = matmuls[r] + [(m, q, g) for m, q in rest[: WHOLE[r]] for g in range(PASSES)]
+        rest = rest[WHOLE[r] :]
+
+    with ExitStack() as ctx:
+        keep = ctx.enter_context(tc.tile_pool(name="keep", bufs=1))
+        stage = ctx.enter_context(tc.tile_pool(name="stage", bufs=4))
+        psum = ctx.enter_context(tc.psum_pool(name="psum", bufs=4))
+        ctx.enter_context(tc.manual_schedule())
+
+        ident = keep.tile([P, P], F32, name="ident")
+        make_identity(nc, ident[:])
+
+        ident_bf = keep.tile([P, P], BF16, name="ident_bf")
+        nc.vector.tensor_copy(out=ident_bf[:], in_=ident[:])
+        folded = keep.tile([P, FOLD], BF16, name="folded")
+        for j, vec in enumerate((b_mu_d, b_ls_d)):
+            nc.sync.dma_start(out=folded[j * P // 2 : (j + 1) * P // 2, :], in_=vec.rearrange("(p e) -> p e", e=FOLD))
+        bias = keep.tile([P, 2, XO], F32, name="bias")
+
+        def spread_bias(b):
+            spread = psum.tile([P, 4, P], F32, name="acc")
+            for i in range(4):
+                e = 4 * b + i
+                nc.tensor.matmul(out=spread[:, i, :], lhsT=folded[:, e : e + 1].to_broadcast([P, P]), rhs=ident_bf[:], start=True, stop=True)
+            dst = bias[:].rearrange("p j (n e) -> p (j n) e", e=FOLD)[:, :, 4 * b : 4 * b + 4]
+            nc.scalar.copy(out=dst, in_=spread[:].rearrange("p e n -> p n e"))
+
+        eps = {}
+        words = {}
+
+        def load_strip(strip, first, count):
+            ks = slice(first * K_PASS, (first + count) * K_PASS)
+            if count == 1:
+                raw = keep.tile([P, TILES, K_PASS], BF16, name="raw_%s_%d" % (strip, first))
+            else:
+                raw = stage.tile([P, TILES, count * K_PASS], BF16, name="raw")
+            i = int(strip[1])
+            if strip[0] == "h":
+                rows = hd[i * STRIP : (i + 1) * STRIP, ks]
+                nc.sync.dma_start(out=raw[:], in_=rows.rearrange("(t p) k -> p t k", p=P))
+            else:
+                for j, weight in enumerate((W_mu_d, W_ls_d)):
+                    rows = weight[i * COLS : (i + 1) * COLS, ks]
+                    nc.sync.dma_start(out=raw[:, 2 * j : 2 * j + 2, :], in_=rows.rearrange("(t p) k -> p t k", p=P))
+            for c in range(count):
+                words[(strip, first + c)] = raw[:].bitcast(F32)[:, :, c * WORDS : (c + 1) * WORDS]
+
+        def load_eps(i, half):
+            cols = slice(half * STRIP, (half + 1) * STRIP)
+            rows = eps_x[i * STRIP : (i + 1) * STRIP, cols]
+            eps[(i, half)] = keep.tile([P, TILES, STRIP], BF16, name="eps_%d_%d" % (i, half))
+            nc.sync.dma_start(out=eps[(i, half)][:], in_=rows.rearrange("(t p) x -> p t x", p=P))
+
+        for g in range(PASSES):
+            load_strip("w0", g, 1)
+            load_strip("h0", g, 1)
+        load_strip("w1", 0, 2)
+        load_strip("w1", 2, 2)
+        load_eps(0, 0)
+        load_strip("h1", 0, 2)
+        load_strip("h1", 2, 2)
+        load_eps(1, 0)
+        late_loads = {
+            5: [lambda: load_strip("w2", 0, 2)],
+            6: [lambda: load_strip("w2", 2, 2), lambda: load_eps(0, 1)],
+            7: [lambda: load_strip("w3", 0, 2)],
+            8: [lambda: load_strip("w3", 2, 2), lambda: load_eps(1, 1)],
+        }
+
+        sorted_words = {}
+        codes, scales = {}, {}
+        acc = {}
+        summed, exped, scaled, finished = [], [], [], []
+
+        def sort_words(piece, engine, half):
+            if half == 0:
+                sorted_words[piece] = stage.tile([P, TILES, 2, P], F32, name="sorted", bufs=4)
+            ts = slice(2 * half, 2 * half + 2)
+            src = words[piece][:, ts, :].rearrange("p t (w u) -> p t u w", u=2)
+            if engine == "vector":
+                nc.vector.tensor_copy(out=sorted_words[piece][:, ts, :, :], in_=src)
+            else:
+                nc.scalar.copy(out=sorted_words[piece][:, ts, :, :], in_=src)
+
+        def transpose_half(piece, grouped, half):
+            bank = psum.tile([P, 2, 2, P], F32, name="xt")
+            for t in range(2):
+                for u in range(2):
+                    if piece in sorted_words:
+                        src = sorted_words[piece][:, 2 * half + t, u, :]
+                    else:
+                        src = words[piece][:, 2 * half + t, u : WORDS : 2]
+                    nc.tensor.transpose(bank[:, t, u, :], src, ident[:])
+            dst = grouped[:].bitcast(F32)[:, half * STRIP : (half + 1) * STRIP]
+            nc.scalar.copy(out=dst.rearrange("p (t r u) -> p t r u", t=2, u=2), in_=bank[:].rearrange("p t u r -> p t r u"))
+
+        def quantize(piece, grouped):
+            codes[piece] = keep.tile([P, STRIP], U32, name="codes_%s_%d" % piece, align_bytes=64)
+            scales[piece] = keep.tile([P, STRIP], U8, name="scales_%s_%d" % piece, align_bytes=64)
+            fmt = E5M2X4 if piece[0][0] == "h" else E4M3X4
+            nc.vector.quantize_mx(out=codes[piece][:].bitcast(fmt), scales=scales[piece][:], in_=grouped[:])
+
+        def multiply(m, q, g):
+            if g == 0:
+                acc[(m, q)] = psum.tile([P, STRIP], F32, name="acc")
+            h_piece, w_piece = ("h%d" % (m // TILES), g), ("w%d" % q, g)
+            rows = slice((m % TILES) * P, (m % TILES + 1) * P)
+            nc.tensor.matmul_mx(
+                out=acc[(m, q)][:],
+                lhsT=codes[h_piece][:, rows].bitcast(E5M2X4),
+                lhsT_scale=scales[h_piece][:, rows],
+                rhs=codes[w_piece][:].bitcast(E4M3X4),
+                rhs_scale=scales[w_piece][:],
+                start=(g == 0),
+                stop=(g == PASSES - 1),
+            )
+
+        def add_bias(m, q):
+            mu_ls = stage.tile([P, STRIP], F32, name="mu_ls", bufs=8)
+            nc.vector.tensor_tensor(
+                out=mu_ls[:].rearrange("p (j c) -> p j c", j=2),
+                in0=acc[(m, q)][:].rearrange("p (j c) -> p j c", j=2),
+                in1=bias[:, :, q * COLS : (q + 1) * COLS],
+                op=ADD,
+            )
+            summed.append((m, q, mu_ls))
+
+        def store(m, q, result):
+            nc.sync.dma_start(out=out[m * P : (m + 1) * P, q * COLS : (q + 1) * COLS], in_=result[:])
+
+        def exponentiate(leave):
+            while len(summed) > leave:
+                m, q, mu_ls = summed.pop(0)
+                std = stage.tile([P, COLS], F32, name="std", bufs=6)
+                nc.scalar.activation(out=std[:], in_=mu_ls[:, COLS:], func=EXP, scale=0.5)
+                exped.append((m, q, mu_ls, std))
+
+        def combine():
+            ready = scaled.pop(0) if scaled else None
+            if exped:
+                m, q, mu_ls, std = exped.pop(0)
+                noise = stage.tile([P, COLS], F32, name="noise")
+                nc.vector.tensor_tensor(out=noise[:], in0=std[:], in1=eps[(m // TILES, q // 2)][:, m % TILES, (q % 2) * COLS : (q % 2 + 1) * COLS], op=MULT)
+                scaled.append((m, q, mu_ls, noise))
+            if ready:
+                m, q, mu_ls, noise = ready
+                result = stage.tile([P, COLS], F32, name="result", bufs=OUT_BUFS)
+                nc.vector.tensor_tensor(out=result[:], in0=mu_ls[:, :COLS], in1=noise[:], op=ADD)
+                finished.append((m, q, result))
+            if not late_loads:
+                for item in finished:
+                    store(*item)
+                finished.clear()
+
+        for r, run in enumerate(runs):
+            for load in late_loads.pop(r, []):
+                load()
+            ahead = runs[r + 1] if r + 1 < len(runs) else []
+            sorts = {"": [], "vector": [], "scalar": []}
+            for j, piece in enumerate(ahead):
+                engine = (SORTER, SORTER2)[j][r + 1]
+                sorts[engine].extend([(piece, engine, half) for half in range(2)])
+            grouped = []
+            for j, piece in enumerate(run):
+                grouped.append(stage.tile([P, 4 * STRIP], BF16, name="grouped", align_bytes=64))
+                if r == 0:
+                    spread_bias(2 * j)
+                    spread_bias(2 * j + 1)
+                for half in range(2):
+                    transpose_half(piece, grouped[j], half)
+                combine()
+                if j == 0:
+                    quantize(piece, grouped[j])
+            for job in sorts["vector"]:
+                sort_words(*job)
+            exponentiate(0)
+            closes = [i for i, (m, q, g) in enumerate(matmuls[r]) if g == PASSES - 1]
+            if not closes or r < 5:
+                quantize(run[1], grouped[1])
+            for i, (m, q, g) in enumerate(matmuls[r]):
+                if i % 4 < SPT and sorts["scalar"]:
+                    sort_words(*sorts["scalar"].pop(0))
+                multiply(m, q, g)
+                if g == PASSES - 1:
+                    add_bias(m, q)
+                    if i == closes[0] and r >= 5:
+                        quantize(run[1], grouped[1])
+                if i % 4 == 3:
+                    if i + 1 < len(matmuls[r]):
+                        exponentiate(1)
+                    combine()
+            for job in sorts["scalar"]:
+                sort_words(*job)
+        exponentiate(0)
+        for i in range(4):
+            combine()

@@ -20,35 +20,44 @@ P = 128
 K_PASS = 512
 PASSES = K // K_PASS
 WORDS = K_PASS // 2
-STRIP = 512
-TILES = STRIP // P
-COLS = STRIP // 2
+TILES = B // P
+STRIPS = XO // P
+BANK = 512
+FOLD = 2 * XO // P
 
-SORTER = [""] + ["vector"] * 8 + ["scalar"] * 3
-SORTER2 = [""] + ["vector"] * 4 + [""] * 4 + ["scalar"] * 3
-WHOLE = {8: 2, 9: 4, 10: 4, 11: 10}
-OUT_BUFS = 18
-SPT = 1
-FOLD = 16
+SORTER = [""] + ["vector"] * 4 + [""] * 2 + ["scalar"] * 5
+SORTER2 = [""] + ["vector"] * 4 + ["scalar"] * 7
+EXTRA = [0] * 7 + [1] * 5
+OUT_BUFS = 16
+SCALE_FROM = 4
+Q_LATE_FROM = 4
+FIRST2 = 1
+RAW_BUFS = 6
+EPS_AFTER = {3: (0, 0), 4: (1, 0), 5: (2, 0), 7: (3, 0), 8: (None, 1)}
 
 
 def tile_vae_pb_kernel(tc, hd, W_mu_d, b_mu_d, W_ls_d, b_ls_d, eps_x, out):
     nc = tc.nc
 
-    runs = [[("w0", g), ("h0", g)] for g in range(PASSES)]
-    for strip in ("w1", "h1", "w2", "w3"):
-        runs.extend([[(strip, 0), (strip, 1)], [(strip, 2), (strip, 3)]])
+    runs = [[("w", 0, 0), ("h", 0, 0)], [("w", 0, 1), ("h", 1, 0)]]
+    for i in range(1, TILES // 2):
+        runs.append([("w", i, 0), ("w", i, 1)])
+        runs.append([("h", 2 * i, 0), ("h", 2 * i + 1, 0)])
+    runs.extend([[("w", s, 0), ("w", s, 1)] for s in range(TILES // 2, STRIPS)])
 
-    matmuls = [[] for r in runs]
-    for g in range(PASSES):
-        matmuls[g + 1] = [(m, 0, g) for m in range(TILES)]
-    for first, rows, q in ((5, range(TILES), 1), (7, range(TILES, 2 * TILES), 0)):
-        for half in range(2):
-            matmuls[first + half] = [(m, q, g) for m in rows for g in (2 * half, 2 * half + 1)]
-    rest = [(m, 1) for m in range(TILES, 2 * TILES)] + [(m, q) for q in (2, 3) for m in range(2 * TILES)]
-    for r in sorted(WHOLE):
-        matmuls[r] = matmuls[r] + [(m, q, g) for m, q in rest[: WHOLE[r]] for g in range(PASSES)]
-        rest = rest[WHOLE[r] :]
+    units = [(0, 0)]
+    ready = [0, 1]
+    for i in range(1, TILES // 2):
+        units.extend([(pair, i) for pair in range(i)])
+        ready.append(len(units))
+        units.extend([(i, s) for s in range(i + 1)])
+        ready.append(len(units))
+    for s in range(TILES // 2, STRIPS):
+        units.extend([(pair, s) for pair in range(TILES // 2)])
+        ready.append(len(units))
+    passes = [(pair, s, t, g) for pair, s in units for t in range(2) for g in range(PASSES)]
+    ends = [0, 2] + [8 * (ready[r - 1] + EXTRA[r]) for r in range(2, len(runs) - 1)] + [len(passes)]
+    matmuls = [passes[ends[r - 1] if r else 0 : ends[r]] for r in range(len(runs))]
 
     with ExitStack() as ctx:
         keep = ctx.enter_context(tc.tile_pool(name="keep", bufs=1))
@@ -58,7 +67,6 @@ def tile_vae_pb_kernel(tc, hd, W_mu_d, b_mu_d, W_ls_d, b_ls_d, eps_x, out):
 
         ident = keep.tile([P, P], F32, name="ident")
         make_identity(nc, ident[:])
-
         ident_bf = keep.tile([P, P], BF16, name="ident_bf")
         nc.vector.tensor_copy(out=ident_bf[:], in_=ident[:])
         folded = keep.tile([P, FOLD], BF16, name="folded")
@@ -74,172 +82,165 @@ def tile_vae_pb_kernel(tc, hd, W_mu_d, b_mu_d, W_ls_d, b_ls_d, eps_x, out):
             dst = bias[:].rearrange("p j (n e) -> p (j n) e", e=FOLD)[:, :, 4 * b : 4 * b + 4]
             nc.scalar.copy(out=dst, in_=spread[:].rearrange("p e n -> p n e"))
 
-        eps = {}
+        eps = [keep.tile([P, TILES, XO // 2], BF16, name="eps_%d" % half) for half in range(2)]
         words = {}
 
-        def load_strip(strip, first, count):
-            ks = slice(first * K_PASS, (first + count) * K_PASS)
-            if count == 1:
-                raw = keep.tile([P, TILES, K_PASS], BF16, name="raw_%s_%d" % (strip, first))
-            else:
-                raw = stage.tile([P, TILES, count * K_PASS], BF16, name="raw")
-            i = int(strip[1])
-            if strip[0] == "h":
-                rows = hd[i * STRIP : (i + 1) * STRIP, ks]
-                nc.sync.dma_start(out=raw[:], in_=rows.rearrange("(t p) k -> p t k", p=P))
+        def load_run(r):
+            raw = stage.tile([P, 2, K], BF16, name="raw", bufs=RAW_BUFS)
+            (kind0, i0, half0), (kind1, i1, half1) = runs[r]
+            if kind0 == kind1 == "h":
+                nc.sync.dma_start(out=raw[:], in_=hd[i0 * P : (i0 + 2) * P, :].rearrange("(t p) k -> p t k", p=P))
+            elif kind0 == kind1:
+                for j, weight in enumerate((W_mu_d, W_ls_d)):
+                    nc.sync.dma_start(out=raw[:, j, :], in_=weight[i0 * P : (i0 + 1) * P, :])
             else:
                 for j, weight in enumerate((W_mu_d, W_ls_d)):
-                    rows = weight[i * COLS : (i + 1) * COLS, ks]
-                    nc.sync.dma_start(out=raw[:, 2 * j : 2 * j + 2, :], in_=rows.rearrange("(t p) k -> p t k", p=P))
-            for c in range(count):
-                words[(strip, first + c)] = raw[:].bitcast(F32)[:, :, c * WORDS : (c + 1) * WORDS]
-
-        def load_eps(i, half):
-            cols = slice(half * STRIP, (half + 1) * STRIP)
-            rows = eps_x[i * STRIP : (i + 1) * STRIP, cols]
-            eps[(i, half)] = keep.tile([P, TILES, STRIP], BF16, name="eps_%d_%d" % (i, half))
-            nc.sync.dma_start(out=eps[(i, half)][:], in_=rows.rearrange("(t p) x -> p t x", p=P))
-
-        for g in range(PASSES):
-            load_strip("w0", g, 1)
-            load_strip("h0", g, 1)
-        load_strip("w1", 0, 2)
-        load_strip("w1", 2, 2)
-        load_eps(0, 0)
-        load_strip("h1", 0, 2)
-        load_strip("h1", 2, 2)
-        load_eps(1, 0)
-        late_loads = {
-            5: [lambda: load_strip("w2", 0, 2)],
-            6: [lambda: load_strip("w2", 2, 2), lambda: load_eps(0, 1)],
-            7: [lambda: load_strip("w3", 0, 2)],
-            8: [lambda: load_strip("w3", 2, 2), lambda: load_eps(1, 1)],
-        }
+                    ks = slice(half0 * K // 2, (half0 + 1) * K // 2)
+                    nc.sync.dma_start(out=raw[:, 0, j * K // 2 : (j + 1) * K // 2], in_=weight[i0 * P : (i0 + 1) * P, ks])
+                nc.sync.dma_start(out=raw[:, 1, :], in_=hd[i1 * P : (i1 + 1) * P, :])
+            view = raw[:].bitcast(F32)
+            for j, piece in enumerate(runs[r]):
+                if piece[0] == "h":
+                    words[piece] = view[:, j, :].rearrange("p (a b w) -> p a b w", a=2, b=2)
+                elif kind0 == kind1:
+                    words[piece] = view[:, :, j * BANK : (j + 1) * BANK].rearrange("p b (a w) -> p a b w", a=2)
+                else:
+                    words[piece] = view[:, j, :].rearrange("p (b a w) -> p a b w", a=2, b=2)
+            if r in EPS_AFTER:
+                pair, half = EPS_AFTER[r]
+                ts = slice(0, TILES) if pair is None else slice(2 * pair, 2 * pair + 2)
+                rows = eps_x[ts.start * P : ts.stop * P, half * XO // 2 : (half + 1) * XO // 2]
+                nc.sync.dma_start(out=eps[half][:, ts, :], in_=rows.rearrange("(t p) x -> p t x", p=P))
 
         sorted_words = {}
         codes, scales = {}, {}
         acc = {}
         summed, exped, scaled, finished = [], [], [], []
 
-        def sort_words(piece, engine, half):
-            if half == 0:
-                sorted_words[piece] = stage.tile([P, TILES, 2, P], F32, name="sorted", bufs=4)
-            ts = slice(2 * half, 2 * half + 2)
-            src = words[piece][:, ts, :].rearrange("p t (w u) -> p t u w", u=2)
+        def sort_words(piece, engine, a):
+            if a == 0:
+                sorted_words[piece] = stage.tile([P, 2, 2, 2, P], F32, name="sorted")
+            src = words[piece][:, a, :, :].rearrange("p b (w u) -> p b u w", u=2)
             if engine == "vector":
-                nc.vector.tensor_copy(out=sorted_words[piece][:, ts, :, :], in_=src)
+                nc.vector.tensor_copy(out=sorted_words[piece][:, a, :, :, :], in_=src)
             else:
-                nc.scalar.copy(out=sorted_words[piece][:, ts, :, :], in_=src)
+                nc.scalar.copy(out=sorted_words[piece][:, a, :, :, :], in_=src)
 
-        def transpose_half(piece, grouped, half):
+        def transpose_half(piece, grouped, a):
             bank = psum.tile([P, 2, 2, P], F32, name="xt")
-            for t in range(2):
+            for b in range(2):
                 for u in range(2):
                     if piece in sorted_words:
-                        src = sorted_words[piece][:, 2 * half + t, u, :]
+                        src = sorted_words[piece][:, a, b, u, :]
                     else:
-                        src = words[piece][:, 2 * half + t, u : WORDS : 2]
-                    nc.tensor.transpose(bank[:, t, u, :], src, ident[:])
-            dst = grouped[:].bitcast(F32)[:, half * STRIP : (half + 1) * STRIP]
-            nc.scalar.copy(out=dst.rearrange("p (t r u) -> p t r u", t=2, u=2), in_=bank[:].rearrange("p t u r -> p t r u"))
+                        src = words[piece][:, a, b, u : WORDS : 2]
+                    nc.tensor.transpose(bank[:, b, u, :], src, ident[:])
+            dst = grouped[:].bitcast(F32)[:, a * BANK : (a + 1) * BANK]
+            nc.scalar.copy(out=dst.rearrange("p (b r u) -> p b r u", b=2, u=2), in_=bank[:].rearrange("p b u r -> p b r u"))
 
         def quantize(piece, grouped):
-            codes[piece] = keep.tile([P, STRIP], U32, name="codes_%s_%d" % piece, align_bytes=64)
-            scales[piece] = keep.tile([P, STRIP], U8, name="scales_%s_%d" % piece, align_bytes=64)
-            fmt = E5M2X4 if piece[0][0] == "h" else E4M3X4
+            codes[piece] = keep.tile([P, BANK], U32, name="codes_%s_%d_%d" % piece, align_bytes=64)
+            scales[piece] = keep.tile([P, BANK], U8, name="scales_%s_%d_%d" % piece, align_bytes=64)
+            fmt = E5M2X4 if piece[0] == "h" else E4M3X4
             nc.vector.quantize_mx(out=codes[piece][:].bitcast(fmt), scales=scales[piece][:], in_=grouped[:])
 
-        def multiply(m, q, g):
-            if g == 0:
-                acc[(m, q)] = psum.tile([P, STRIP], F32, name="acc")
-            h_piece, w_piece = ("h%d" % (m // TILES), g), ("w%d" % q, g)
-            rows = slice((m % TILES) * P, (m % TILES + 1) * P)
+        def multiply(pair, s, t, g):
+            if (t, g) == (0, 0):
+                acc[(pair, s)] = psum.tile([P, 2, 2 * P], F32, name="acc")
+            h_piece, w_piece = ("h", 2 * pair + t, 0), ("w", s, g // 2)
+            rows = slice(g * P, (g + 1) * P)
+            cols = slice((g % 2) * 2 * P, (g % 2 + 1) * 2 * P)
             nc.tensor.matmul_mx(
-                out=acc[(m, q)][:],
+                out=acc[(pair, s)][:, t, :],
                 lhsT=codes[h_piece][:, rows].bitcast(E5M2X4),
                 lhsT_scale=scales[h_piece][:, rows],
-                rhs=codes[w_piece][:].bitcast(E4M3X4),
-                rhs_scale=scales[w_piece][:],
+                rhs=codes[w_piece][:, cols].bitcast(E4M3X4),
+                rhs_scale=scales[w_piece][:, cols],
                 start=(g == 0),
                 stop=(g == PASSES - 1),
             )
 
-        def add_bias(m, q):
-            mu_ls = stage.tile([P, STRIP], F32, name="mu_ls", bufs=8)
+        def add_bias(pair, s):
+            mu_ls = stage.tile([P, 2, 2, P], F32, name="mu_ls", bufs=8)
             nc.vector.tensor_tensor(
-                out=mu_ls[:].rearrange("p (j c) -> p j c", j=2),
-                in0=acc[(m, q)][:].rearrange("p (j c) -> p j c", j=2),
-                in1=bias[:, :, q * COLS : (q + 1) * COLS],
+                out=mu_ls[:],
+                in0=acc[(pair, s)][:].rearrange("p t (j c) -> p t j c", j=2),
+                in1=bias[:, :, s * P : (s + 1) * P].unsqueeze(1).to_broadcast([P, 2, 2, P]),
                 op=ADD,
             )
-            summed.append((m, q, mu_ls))
+            summed.append((pair, s, mu_ls))
 
-        def store(m, q, result):
-            nc.sync.dma_start(out=out[m * P : (m + 1) * P, q * COLS : (q + 1) * COLS], in_=result[:])
+        def exponentiate():
+            for pair, s, mu_ls in summed:
+                std = stage.tile([P, 2, P], F32, name="std", bufs=6)
+                nc.scalar.activation(out=std[:], in_=mu_ls[:, :, 1, :], func=EXP, scale=0.5)
+                exped.append((pair, s, mu_ls, std))
+            summed.clear()
 
-        def exponentiate(leave):
-            while len(summed) > leave:
-                m, q, mu_ls = summed.pop(0)
-                std = stage.tile([P, COLS], F32, name="std", bufs=6)
-                nc.scalar.activation(out=std[:], in_=mu_ls[:, COLS:], func=EXP, scale=0.5)
-                exped.append((m, q, mu_ls, std))
-
-        def combine():
+        def combine(may_scale, may_store):
             ready = scaled.pop(0) if scaled else None
-            if exped:
-                m, q, mu_ls, std = exped.pop(0)
-                noise = stage.tile([P, COLS], F32, name="noise")
-                nc.vector.tensor_tensor(out=noise[:], in0=std[:], in1=eps[(m // TILES, q // 2)][:, m % TILES, (q % 2) * COLS : (q % 2 + 1) * COLS], op=MULT)
-                scaled.append((m, q, mu_ls, noise))
+            if exped and may_scale:
+                pair, s, mu_ls, std = exped.pop(0)
+                noise = stage.tile([P, 2, P], F32, name="noise")
+                half, c = divmod(s * P, XO // 2)
+                nc.vector.tensor_tensor(out=noise[:], in0=std[:], in1=eps[half][:, 2 * pair : 2 * pair + 2, c : c + P], op=MULT)
+                scaled.append((pair, s, mu_ls, noise))
             if ready:
-                m, q, mu_ls, noise = ready
-                result = stage.tile([P, COLS], F32, name="result", bufs=OUT_BUFS)
-                nc.vector.tensor_tensor(out=result[:], in0=mu_ls[:, :COLS], in1=noise[:], op=ADD)
-                finished.append((m, q, result))
-            if not late_loads:
-                for item in finished:
-                    store(*item)
+                pair, s, mu_ls, noise = ready
+                result = stage.tile([P, 2, P], F32, name="result", bufs=OUT_BUFS)
+                nc.vector.tensor_tensor(out=result[:], in0=mu_ls[:, :, 0, :], in1=noise[:], op=ADD)
+                finished.append((pair, s, result))
+            if may_store:
+                for pair, s, result in finished:
+                    rows = out[2 * pair * P : (2 * pair + 2) * P, s * P : (s + 1) * P]
+                    nc.sync.dma_start(out=rows.rearrange("(t p) x -> p t x", p=P), in_=result[:])
                 finished.clear()
 
+        for r in range(RAW_BUFS):
+            load_run(r)
         for r, run in enumerate(runs):
-            for load in late_loads.pop(r, []):
-                load()
+            if 0 < r <= len(runs) - RAW_BUFS:
+                load_run(r + RAW_BUFS - 1)
+            may_scale = r >= SCALE_FROM
+            may_store = r >= len(runs) - RAW_BUFS
             ahead = runs[r + 1] if r + 1 < len(runs) else []
             sorts = {"": [], "vector": [], "scalar": []}
             for j, piece in enumerate(ahead):
                 engine = (SORTER, SORTER2)[j][r + 1]
-                sorts[engine].extend([(piece, engine, half) for half in range(2)])
+                sorts[engine].extend([(piece, engine, a) for a in range(2)])
             grouped = []
             for j, piece in enumerate(run):
-                grouped.append(stage.tile([P, 4 * STRIP], BF16, name="grouped", align_bytes=64))
+                grouped.append(stage.tile([P, 4 * BANK], BF16, name="grouped", align_bytes=64))
                 if r == 0:
                     spread_bias(2 * j)
                     spread_bias(2 * j + 1)
-                for half in range(2):
-                    transpose_half(piece, grouped[j], half)
-                combine()
+                for a in range(2):
+                    transpose_half(piece, grouped[j], a)
+                combine(may_scale, may_store)
                 if j == 0:
                     quantize(piece, grouped[j])
             for job in sorts["vector"]:
                 sort_words(*job)
-            exponentiate(0)
-            closes = [i for i, (m, q, g) in enumerate(matmuls[r]) if g == PASSES - 1]
-            if not closes or r < 5:
+            early = r < Q_LATE_FROM
+            if early:
                 quantize(run[1], grouped[1])
-            for i, (m, q, g) in enumerate(matmuls[r]):
-                if i % 4 < SPT and sorts["scalar"]:
-                    sort_words(*sorts["scalar"].pop(0))
-                multiply(m, q, g)
-                if g == PASSES - 1:
-                    add_bias(m, q)
-                    if i == closes[0] and r >= 5:
+            exponentiate()
+            for i, (pair, s, t, g) in enumerate(matmuls[r]):
+                if i % 8 == 0:
+                    if sorts["scalar"]:
+                        sort_words(*sorts["scalar"].pop(0))
+                        if i == 0 and FIRST2 and sorts["scalar"]:
+                            sort_words(*sorts["scalar"].pop(0))
+                    exponentiate()
+                multiply(pair, s, t, g)
+                if (t, g) == (1, PASSES - 1):
+                    add_bias(pair, s)
+                    if not early:
                         quantize(run[1], grouped[1])
-                if i % 4 == 3:
-                    if i + 1 < len(matmuls[r]):
-                        exponentiate(1)
-                    combine()
+                        early = True
+                    combine(may_scale, may_store)
             for job in sorts["scalar"]:
                 sort_words(*job)
-        exponentiate(0)
+        exponentiate()
         for i in range(4):
-            combine()
+            combine(True, True)

@@ -25,15 +25,17 @@ STRIPS = XO // P
 BANK = 512
 FOLD = 2 * XO // P
 
-SORTER = [""] + ["vector"] * 4 + [""] * 2 + ["scalar"] * 5
-SORTER2 = [""] + ["vector"] * 4 + ["scalar"] * 7
+SORTER = [""] * 2 + ["vector"] * 3 + [""] * 7
+SORTER2 = [""] * 2 + ["vector"] * 3 + ["scalar"] * 7
 EXTRA = [0] * 7 + [1] * 5
 OUT_BUFS = 16
 SCALE_FROM = 4
 Q_LATE_FROM = 4
 FIRST2 = 1
+BIAS_AT = [[0, 1, 2, 3], []]
+SPLIT = 1
 RAW_BUFS = 6
-EPS_AFTER = {3: (0, 0), 4: (1, 0), 5: (2, 0), 7: (3, 0), 8: (None, 1)}
+EPS_AFTER = {4: (0, 0), 5: (1, 0), 6: (2, 0), 7: (3, 0), 8: (None, 1)}
 
 
 def tile_vae_pb_kernel(tc, hd, W_mu_d, b_mu_d, W_ls_d, b_ls_d, eps_x, out):
@@ -55,7 +57,11 @@ def tile_vae_pb_kernel(tc, hd, W_mu_d, b_mu_d, W_ls_d, b_ls_d, eps_x, out):
     for s in range(TILES // 2, STRIPS):
         units.extend([(pair, s) for pair in range(TILES // 2)])
         ready.append(len(units))
-    passes = [(pair, s, t, g) for pair, s in units for t in range(2) for g in range(PASSES)]
+    units = [(2 * pair, 2, s) for pair, s in units]
+    for m, count, s in units[len(units) - SPLIT :]:
+        units.remove((m, count, s))
+        units.extend([(m, 1, s), (m + 1, 1, s)])
+    passes = [(unit, t, g) for unit in units for t in range(unit[1]) for g in range(PASSES)]
     ends = [0, 2] + [8 * (ready[r - 1] + EXTRA[r]) for r in range(2, len(runs) - 1)] + [len(passes)]
     matmuls = [passes[ends[r - 1] if r else 0 : ends[r]] for r in range(len(runs))]
 
@@ -80,7 +86,7 @@ def tile_vae_pb_kernel(tc, hd, W_mu_d, b_mu_d, W_ls_d, b_ls_d, eps_x, out):
                 e = 4 * b + i
                 nc.tensor.matmul(out=spread[:, i, :], lhsT=folded[:, e : e + 1].to_broadcast([P, P]), rhs=ident_bf[:], start=True, stop=True)
             dst = bias[:].rearrange("p j (n e) -> p (j n) e", e=FOLD)[:, :, 4 * b : 4 * b + 4]
-            nc.scalar.copy(out=dst, in_=spread[:].rearrange("p e n -> p n e"))
+            nc.vector.tensor_copy(out=dst, in_=spread[:].rearrange("p e n -> p n e"))
 
         eps = [keep.tile([P, TILES, XO // 2], BF16, name="eps_%d" % half) for half in range(2)]
         words = {}
@@ -144,14 +150,15 @@ def tile_vae_pb_kernel(tc, hd, W_mu_d, b_mu_d, W_ls_d, b_ls_d, eps_x, out):
             fmt = E5M2X4 if piece[0] == "h" else E4M3X4
             nc.vector.quantize_mx(out=codes[piece][:].bitcast(fmt), scales=scales[piece][:], in_=grouped[:])
 
-        def multiply(pair, s, t, g):
+        def multiply(unit, t, g):
+            m, count, s = unit
             if (t, g) == (0, 0):
-                acc[(pair, s)] = psum.tile([P, 2, 2 * P], F32, name="acc")
-            h_piece, w_piece = ("h", 2 * pair + t, 0), ("w", s, g // 2)
+                acc[unit] = psum.tile([P, count, 2 * P], F32, name="acc")
+            h_piece, w_piece = ("h", m + t, 0), ("w", s, g // 2)
             rows = slice(g * P, (g + 1) * P)
             cols = slice((g % 2) * 2 * P, (g % 2 + 1) * 2 * P)
             nc.tensor.matmul_mx(
-                out=acc[(pair, s)][:, t, :],
+                out=acc[unit][:, t, :],
                 lhsT=codes[h_piece][:, rows].bitcast(E5M2X4),
                 lhsT_scale=scales[h_piece][:, rows],
                 rhs=codes[w_piece][:, cols].bitcast(E4M3X4),
@@ -160,39 +167,41 @@ def tile_vae_pb_kernel(tc, hd, W_mu_d, b_mu_d, W_ls_d, b_ls_d, eps_x, out):
                 stop=(g == PASSES - 1),
             )
 
-        def add_bias(pair, s):
-            mu_ls = stage.tile([P, 2, 2, P], F32, name="mu_ls", bufs=8)
+        def add_bias(unit):
+            m, count, s = unit
+            mu_ls = stage.tile([P, count, 2, P], F32, name="mu_ls", bufs=8)
             nc.vector.tensor_tensor(
                 out=mu_ls[:],
-                in0=acc[(pair, s)][:].rearrange("p t (j c) -> p t j c", j=2),
-                in1=bias[:, :, s * P : (s + 1) * P].unsqueeze(1).to_broadcast([P, 2, 2, P]),
+                in0=acc[unit][:].rearrange("p t (j c) -> p t j c", j=2),
+                in1=bias[:, :, s * P : (s + 1) * P].unsqueeze(1).to_broadcast([P, count, 2, P]),
                 op=ADD,
             )
-            summed.append((pair, s, mu_ls))
+            summed.append((unit, mu_ls))
 
         def exponentiate():
-            for pair, s, mu_ls in summed:
-                std = stage.tile([P, 2, P], F32, name="std", bufs=6)
+            for unit, mu_ls in summed:
+                std = stage.tile([P, unit[1], P], F32, name="std", bufs=6)
                 nc.scalar.activation(out=std[:], in_=mu_ls[:, :, 1, :], func=EXP, scale=0.5)
-                exped.append((pair, s, mu_ls, std))
+                exped.append((unit, mu_ls, std))
             summed.clear()
 
         def combine(may_scale, may_store):
             ready = scaled.pop(0) if scaled else None
             if exped and may_scale:
-                pair, s, mu_ls, std = exped.pop(0)
-                noise = stage.tile([P, 2, P], F32, name="noise")
+                unit, mu_ls, std = exped.pop(0)
+                m, count, s = unit
+                noise = stage.tile([P, count, P], F32, name="noise")
                 half, c = divmod(s * P, XO // 2)
-                nc.vector.tensor_tensor(out=noise[:], in0=std[:], in1=eps[half][:, 2 * pair : 2 * pair + 2, c : c + P], op=MULT)
-                scaled.append((pair, s, mu_ls, noise))
+                nc.vector.tensor_tensor(out=noise[:], in0=std[:], in1=eps[half][:, m : m + count, c : c + P], op=MULT)
+                scaled.append((unit, mu_ls, noise))
             if ready:
-                pair, s, mu_ls, noise = ready
-                result = stage.tile([P, 2, P], F32, name="result", bufs=OUT_BUFS)
+                unit, mu_ls, noise = ready
+                result = stage.tile([P, unit[1], P], F32, name="result", bufs=OUT_BUFS)
                 nc.vector.tensor_tensor(out=result[:], in0=mu_ls[:, :, 0, :], in1=noise[:], op=ADD)
-                finished.append((pair, s, result))
+                finished.append((unit, result))
             if may_store:
-                for pair, s, result in finished:
-                    rows = out[2 * pair * P : (2 * pair + 2) * P, s * P : (s + 1) * P]
+                for (m, count, s), result in finished:
+                    rows = out[m * P : (m + count) * P, s * P : (s + 1) * P]
                     nc.sync.dma_start(out=rows.rearrange("(t p) x -> p t x", p=P), in_=result[:])
                 finished.clear()
 
@@ -212,8 +221,8 @@ def tile_vae_pb_kernel(tc, hd, W_mu_d, b_mu_d, W_ls_d, b_ls_d, eps_x, out):
             for j, piece in enumerate(run):
                 grouped.append(stage.tile([P, 4 * BANK], BF16, name="grouped", align_bytes=64))
                 if r == 0:
-                    spread_bias(2 * j)
-                    spread_bias(2 * j + 1)
+                    for b in BIAS_AT[j]:
+                        spread_bias(b)
                 for a in range(2):
                     transpose_half(piece, grouped[j], a)
                 combine(may_scale, may_store)
@@ -225,16 +234,16 @@ def tile_vae_pb_kernel(tc, hd, W_mu_d, b_mu_d, W_ls_d, b_ls_d, eps_x, out):
             if early:
                 quantize(run[1], grouped[1])
             exponentiate()
-            for i, (pair, s, t, g) in enumerate(matmuls[r]):
-                if i % 8 == 0:
+            for i, (unit, t, g) in enumerate(matmuls[r]):
+                if (t, g) == (0, 0):
                     if sorts["scalar"]:
                         sort_words(*sorts["scalar"].pop(0))
                         if i == 0 and FIRST2 and sorts["scalar"]:
                             sort_words(*sorts["scalar"].pop(0))
                     exponentiate()
-                multiply(pair, s, t, g)
-                if (t, g) == (1, PASSES - 1):
-                    add_bias(pair, s)
+                multiply(unit, t, g)
+                if (t, g) == (unit[1] - 1, PASSES - 1):
+                    add_bias(unit)
                     if not early:
                         quantize(run[1], grouped[1])
                         early = True

@@ -17,53 +17,65 @@ MULT = mybir.AluOpType.mult
 EXP = mybir.ActivationFunctionType.Exp
 
 P = 128
-K_PASS = 512
-PASSES = K // K_PASS
-WORDS = K_PASS // 2
-TILES = B // P
-STRIPS = XO // P
+PASSES = K // 512
+WORDS = 256
 BANK = 512
+COLS = 256
+PAIRS = B // (2 * P)
 FOLD = 2 * XO // P
+MU, LS = 0, 1
 
-SORTER = [""] * 2 + ["vector"] * 3 + [""] * 7
-SORTER2 = [""] * 2 + ["vector"] * 3 + ["scalar"] * 7
-EXTRA = [0] * 7 + [1] * 5
-OUT_BUFS = 16
-SCALE_FROM = 4
-Q_LATE_FROM = 4
-FIRST2 = 1
-BIAS_AT = [[0, 1, 2, 3], []]
-SPLIT = 1
+FIRST_SORTED_RUN = 2
+FIRST_SCALAR_RUN = 5
+FIRST_FULL_SCALAR_RUN = 7
+FIRST_BUSY_RUN = 4
+
 RAW_BUFS = 6
-EPS_AFTER = {4: (0, 0), 5: (1, 0), 6: (2, 0), 7: (3, 0), 8: (None, 1)}
+RESULT_BUFS = 8
+SHIFTED_BUFS = 12
+LS_BUFS = 4
+
+
+def sorter(r, j):
+    if r < FIRST_SORTED_RUN or (j == 0 and FIRST_SCALAR_RUN <= r < FIRST_FULL_SCALAR_RUN):
+        return None
+    return "vector" if r < FIRST_SCALAR_RUN else "scalar"
 
 
 def tile_vae_pb_kernel(tc, hd, W_mu_d, b_mu_d, W_ls_d, b_ls_d, eps_x, out):
     nc = tc.nc
 
-    runs = [[("w", 0, 0), ("h", 0, 0)], [("w", 0, 1), ("h", 1, 0)]]
-    for i in range(1, TILES // 2):
-        runs.append([("w", i, 0), ("w", i, 1)])
-        runs.append([("h", 2 * i, 0), ("h", 2 * i + 1, 0)])
-    runs.extend([[("w", s, 0), ("w", s, 1)] for s in range(TILES // 2, STRIPS)])
+    quarters = XO // COLS
+    strips = [(LS, 0)]
+    for q in range(quarters - 1):
+        strips.extend([(LS, q + 1), (MU, q)])
+    strips.append((MU, quarters - 1))
 
-    units = [(0, 0)]
+    runs = [[("w", 0, 0), ("h", 0, 0)], [("w", 0, 1), ("h", 1, 0)]]
+    units = [(0, 2, 0)]
     ready = [0, 1]
-    for i in range(1, TILES // 2):
-        units.extend([(pair, i) for pair in range(i)])
+    for i in range(1, PAIRS):
+        runs.append([("w", i, 0), ("w", i, 1)])
+        units.extend([(2 * pair, 2, i) for pair in range(i)])
         ready.append(len(units))
-        units.extend([(i, s) for s in range(i + 1)])
+        runs.append([("h", 2 * i, 0), ("h", 2 * i + 1, 0)])
+        units.extend([(2 * i, 2, s) for s in sorted(range(i + 1), key=lambda s: strips[s][0] == MU)])
         ready.append(len(units))
-    for s in range(TILES // 2, STRIPS):
-        units.extend([(pair, s) for pair in range(TILES // 2)])
+    for s in range(PAIRS, len(strips)):
+        runs.append([("w", s, 0), ("w", s, 1)])
+        units.extend([(2 * pair, 2, s) for pair in range(PAIRS)])
         ready.append(len(units))
-    units = [(2 * pair, 2, s) for pair, s in units]
-    for m, count, s in units[len(units) - SPLIT :]:
-        units.remove((m, count, s))
-        units.extend([(m, 1, s), (m + 1, 1, s)])
+    m_last, count_last, s_last = units.pop()
+    units.extend([(m_last + t, 1, s_last) for t in range(count_last)])
+
     passes = [(unit, t, g) for unit in units for t in range(unit[1]) for g in range(PASSES)]
-    ends = [0, 2] + [8 * (ready[r - 1] + EXTRA[r]) for r in range(2, len(runs) - 1)] + [len(passes)]
-    matmuls = [passes[ends[r - 1] if r else 0 : ends[r]] for r in range(len(runs))]
+    ends = [0, PASSES // 2] + [2 * PASSES * ready[r - 1] for r in range(2, len(runs) - 1)] + [len(passes)]
+    passes_after = [passes[start:end] for start, end in zip([0] + ends, ends)]
+
+    eps_after = {runs.index([("h", 2 * i, 0), ("h", 2 * i + 1, 0)]): (i, i + 1, 0) for i in range(1, PAIRS)}
+    eps_after[min(eps_after)] = (0, 2, 0)
+    first_right = strips.index((LS, quarters // 2))
+    eps_after[runs.index([("w", first_right, 0), ("w", first_right, 1)])] = (0, PAIRS, 1)
 
     with ExitStack() as ctx:
         keep = ctx.enter_context(tc.tile_pool(name="keep", bufs=1))
@@ -75,53 +87,56 @@ def tile_vae_pb_kernel(tc, hd, W_mu_d, b_mu_d, W_ls_d, b_ls_d, eps_x, out):
         make_identity(nc, ident[:])
         ident_bf = keep.tile([P, P], BF16, name="ident_bf")
         nc.vector.tensor_copy(out=ident_bf[:], in_=ident[:])
+
         folded = keep.tile([P, FOLD], BF16, name="folded")
         for j, vec in enumerate((b_mu_d, b_ls_d)):
             nc.sync.dma_start(out=folded[j * P // 2 : (j + 1) * P // 2, :], in_=vec.rearrange("(p e) -> p e", e=FOLD))
         bias = keep.tile([P, 2, XO], F32, name="bias")
 
-        def spread_bias(b):
-            spread = psum.tile([P, 4, P], F32, name="acc")
-            for i in range(4):
-                e = 4 * b + i
-                nc.tensor.matmul(out=spread[:, i, :], lhsT=folded[:, e : e + 1].to_broadcast([P, P]), rhs=ident_bf[:], start=True, stop=True)
-            dst = bias[:].rearrange("p j (n e) -> p (j n) e", e=FOLD)[:, :, 4 * b : 4 * b + 4]
-            nc.vector.tensor_copy(out=dst, in_=spread[:].rearrange("p e n -> p n e"))
+        def spread_biases():
+            per_bank = BANK // P
+            for e0 in range(0, FOLD, per_bank):
+                spread = psum.tile([P, per_bank, P], F32, name="acc")
+                for i in range(per_bank):
+                    column = folded[:, e0 + i : e0 + i + 1].to_broadcast([P, P])
+                    nc.tensor.matmul(out=spread[:, i, :], lhsT=column, rhs=ident_bf[:], start=True, stop=True)
+                dst = bias[:].rearrange("p j (n e) -> p (j n) e", e=FOLD)[:, :, e0 : e0 + per_bank]
+                nc.vector.tensor_copy(out=dst, in_=spread[:].rearrange("p e n -> p n e"))
 
-        eps = [keep.tile([P, TILES, XO // 2], BF16, name="eps_%d" % half) for half in range(2)]
+        eps = [keep.tile([P, B // P, XO // 2], BF16, name="eps_%d" % half) for half in range(2)]
         words = {}
 
         def load_run(r):
             raw = stage.tile([P, 2, K], BF16, name="raw", bufs=RAW_BUFS)
             (kind0, i0, half0), (kind1, i1, half1) = runs[r]
-            if kind0 == kind1 == "h":
-                nc.sync.dma_start(out=raw[:], in_=hd[i0 * P : (i0 + 2) * P, :].rearrange("(t p) k -> p t k", p=P))
-            elif kind0 == kind1:
-                for j, weight in enumerate((W_mu_d, W_ls_d)):
-                    nc.sync.dma_start(out=raw[:, j, :], in_=weight[i0 * P : (i0 + 1) * P, :])
-            else:
-                for j, weight in enumerate((W_mu_d, W_ls_d)):
-                    ks = slice(half0 * K // 2, (half0 + 1) * K // 2)
-                    nc.sync.dma_start(out=raw[:, 0, j * K // 2 : (j + 1) * K // 2], in_=weight[i0 * P : (i0 + 1) * P, ks])
-                nc.sync.dma_start(out=raw[:, 1, :], in_=hd[i1 * P : (i1 + 1) * P, :])
             view = raw[:].bitcast(F32)
-            for j, piece in enumerate(runs[r]):
-                if piece[0] == "h":
+            if kind0 == "h":
+                nc.sync.dma_start(out=raw[:], in_=hd[i0 * P : (i0 + 2) * P, :].rearrange("(t p) k -> p t k", p=P))
+                for j, piece in enumerate(runs[r]):
                     words[piece] = view[:, j, :].rearrange("p (a b w) -> p a b w", a=2, b=2)
-                elif kind0 == kind1:
-                    words[piece] = view[:, :, j * BANK : (j + 1) * BANK].rearrange("p b (a w) -> p a b w", a=2)
+            else:
+                matrix, q = strips[i0]
+                rows = (W_mu_d, W_ls_d)[matrix][q * COLS : (q + 1) * COLS, :].rearrange("(b p) k -> p b k", p=P)
+                if kind1 == "w":
+                    nc.sync.dma_start(out=raw[:], in_=rows)
+                    for j, piece in enumerate(runs[r]):
+                        words[piece] = view[:, :, j * BANK : (j + 1) * BANK].rearrange("p b (a w) -> p a b w", a=2)
                 else:
-                    words[piece] = view[:, j, :].rearrange("p (b a w) -> p a b w", a=2, b=2)
-            if r in EPS_AFTER:
-                pair, half = EPS_AFTER[r]
-                ts = slice(0, TILES) if pair is None else slice(2 * pair, 2 * pair + 2)
-                rows = eps_x[ts.start * P : ts.stop * P, half * XO // 2 : (half + 1) * XO // 2]
-                nc.sync.dma_start(out=eps[half][:, ts, :], in_=rows.rearrange("(t p) x -> p t x", p=P))
+                    ks = slice(half0 * K // 2, (half0 + 1) * K // 2)
+                    nc.sync.dma_start(out=raw[:, 0, :].rearrange("p (b k) -> p b k", b=2), in_=rows[:, :, ks])
+                    nc.sync.dma_start(out=raw[:, 1, :], in_=hd[i1 * P : (i1 + 1) * P, :])
+                    words[runs[r][0]] = view[:, 0, :].rearrange("p (b a w) -> p a b w", a=2, b=2)
+                    words[runs[r][1]] = view[:, 1, :].rearrange("p (a b w) -> p a b w", a=2, b=2)
+            if r in eps_after:
+                first, end, half = eps_after[r]
+                rows = eps_x[2 * first * P : 2 * end * P, half * XO // 2 : (half + 1) * XO // 2]
+                nc.sync.dma_start(out=eps[half][:, 2 * first : 2 * end, :], in_=rows.rearrange("(t p) x -> p t x", p=P))
 
         sorted_words = {}
         codes, scales = {}, {}
         acc = {}
-        summed, exped, scaled, finished = [], [], [], []
+        shifted = {}
+        closed, summed, exped, scaled, finished = [], [], [], [], []
 
         def sort_words(piece, engine, a):
             if a == 0:
@@ -132,17 +147,17 @@ def tile_vae_pb_kernel(tc, hd, W_mu_d, b_mu_d, W_ls_d, b_ls_d, eps_x, out):
             else:
                 nc.scalar.copy(out=sorted_words[piece][:, a, :, :, :], in_=src)
 
-        def transpose_half(piece, grouped, a):
+        def transpose_bank(piece, grouped, a):
             bank = psum.tile([P, 2, 2, P], F32, name="xt")
             for b in range(2):
                 for u in range(2):
                     if piece in sorted_words:
                         src = sorted_words[piece][:, a, b, u, :]
                     else:
-                        src = words[piece][:, a, b, u : WORDS : 2]
+                        src = words[piece][:, a, b, u:WORDS:2]
                     nc.tensor.transpose(bank[:, b, u, :], src, ident[:])
             dst = grouped[:].bitcast(F32)[:, a * BANK : (a + 1) * BANK]
-            nc.scalar.copy(out=dst.rearrange("p (b r u) -> p b r u", b=2, u=2), in_=bank[:].rearrange("p b u r -> p b r u"))
+            nc.scalar.copy(out=dst.rearrange("p (b c u) -> p b c u", b=2, u=2), in_=bank[:].rearrange("p b u c -> p b c u"))
 
         def quantize(piece, grouped):
             codes[piece] = keep.tile([P, BANK], U32, name="codes_%s_%d_%d" % piece, align_bytes=64)
@@ -153,103 +168,116 @@ def tile_vae_pb_kernel(tc, hd, W_mu_d, b_mu_d, W_ls_d, b_ls_d, eps_x, out):
         def multiply(unit, t, g):
             m, count, s = unit
             if (t, g) == (0, 0):
-                acc[unit] = psum.tile([P, count, 2 * P], F32, name="acc")
+                acc[unit] = psum.tile([P, count, COLS], F32, name="acc")
             h_piece, w_piece = ("h", m + t, 0), ("w", s, g // 2)
-            rows = slice(g * P, (g + 1) * P)
-            cols = slice((g % 2) * 2 * P, (g % 2 + 1) * 2 * P)
+            h_cols = slice(g * P, (g + 1) * P)
+            w_cols = slice((g % 2) * COLS, (g % 2 + 1) * COLS)
             nc.tensor.matmul_mx(
                 out=acc[unit][:, t, :],
-                lhsT=codes[h_piece][:, rows].bitcast(E5M2X4),
-                lhsT_scale=scales[h_piece][:, rows],
-                rhs=codes[w_piece][:, cols].bitcast(E4M3X4),
-                rhs_scale=scales[w_piece][:, cols],
+                lhsT=codes[h_piece][:, h_cols].bitcast(E5M2X4),
+                lhsT_scale=scales[h_piece][:, h_cols],
+                rhs=codes[w_piece][:, w_cols].bitcast(E4M3X4),
+                rhs_scale=scales[w_piece][:, w_cols],
                 start=(g == 0),
                 stop=(g == PASSES - 1),
             )
 
-        def add_bias(unit):
+        def bias_of(matrix, unit):
             m, count, s = unit
-            mu_ls = stage.tile([P, count, 2, P], F32, name="mu_ls", bufs=8)
-            nc.vector.tensor_tensor(
-                out=mu_ls[:],
-                in0=acc[unit][:].rearrange("p t (j c) -> p t j c", j=2),
-                in1=bias[:, :, s * P : (s + 1) * P].unsqueeze(1).to_broadcast([P, count, 2, P]),
-                op=ADD,
-            )
-            summed.append((unit, mu_ls))
+            q = strips[s][1]
+            return bias[:, matrix, q * COLS : (q + 1) * COLS].unsqueeze(1).to_broadcast([P, count, COLS])
+
+        def empty_banks():
+            for unit in list(closed):
+                m, count, s = unit
+                matrix, q = strips[s]
+                t = m % 2
+                if matrix == LS:
+                    ls = stage.tile([P, count, COLS], F32, name="ls", bufs=LS_BUFS)
+                    nc.vector.tensor_tensor(out=ls[:], in0=acc[unit][:], in1=bias_of(LS, unit), op=ADD)
+                    summed.append((unit, ls))
+                    closed.remove(unit)
+                elif (m - t, q) in shifted:
+                    result = stage.tile([P, count, COLS], F32, name="result", bufs=RESULT_BUFS)
+                    nc.vector.tensor_tensor(out=result[:], in0=acc[unit][:], in1=shifted[(m - t, q)][:, t : t + count, :], op=ADD)
+                    finished.append((unit, result))
+                    closed.remove(unit)
 
         def exponentiate():
-            for unit, mu_ls in summed:
-                std = stage.tile([P, unit[1], P], F32, name="std", bufs=6)
-                nc.scalar.activation(out=std[:], in_=mu_ls[:, :, 1, :], func=EXP, scale=0.5)
-                exped.append((unit, mu_ls, std))
+            for unit, ls in summed:
+                std = stage.tile([P, 2, COLS], F32, name="std", bufs=LS_BUFS)
+                nc.scalar.activation(out=std[:], in_=ls[:], func=EXP, scale=0.5)
+                exped.append((unit, std))
             summed.clear()
 
-        def combine(may_scale, may_store):
-            ready = scaled.pop(0) if scaled else None
-            if exped and may_scale:
-                unit, mu_ls, std = exped.pop(0)
+        def shift_step():
+            if scaled:
+                unit, noise = scaled.pop(0)
+                key = (unit[0], strips[unit[2]][1])
+                shifted[key] = stage.tile([P, 2, COLS], F32, name="shifted", bufs=SHIFTED_BUFS)
+                nc.vector.tensor_tensor(out=shifted[key][:], in0=noise[:], in1=bias_of(MU, unit), op=ADD)
+            elif exped:
+                unit, std = exped.pop(0)
                 m, count, s = unit
-                noise = stage.tile([P, count, P], F32, name="noise")
-                half, c = divmod(s * P, XO // 2)
-                nc.vector.tensor_tensor(out=noise[:], in0=std[:], in1=eps[half][:, m : m + count, c : c + P], op=MULT)
-                scaled.append((unit, mu_ls, noise))
-            if ready:
-                unit, mu_ls, noise = ready
-                result = stage.tile([P, unit[1], P], F32, name="result", bufs=OUT_BUFS)
-                nc.vector.tensor_tensor(out=result[:], in0=mu_ls[:, :, 0, :], in1=noise[:], op=ADD)
-                finished.append((unit, result))
-            if may_store:
-                for (m, count, s), result in finished:
-                    rows = out[m * P : (m + count) * P, s * P : (s + 1) * P]
-                    nc.sync.dma_start(out=rows.rearrange("(t p) x -> p t x", p=P), in_=result[:])
-                finished.clear()
+                noise = stage.tile([P, 2, COLS], F32, name="noise", bufs=2)
+                half, c = divmod(strips[s][1] * COLS, XO // 2)
+                nc.vector.tensor_tensor(out=noise[:], in0=std[:], in1=eps[half][:, m : m + 2, c : c + COLS], op=MULT)
+                scaled.append((unit, noise))
+
+        def store():
+            for (m, count, s), result in finished:
+                q = strips[s][1]
+                rows = out[m * P : (m + count) * P, q * COLS : (q + 1) * COLS]
+                nc.sync.dma_start(out=rows.rearrange("(t p) x -> p t x", p=P), in_=result[:])
+            finished.clear()
 
         for r in range(RAW_BUFS):
             load_run(r)
+        spread_biases()
         for r, run in enumerate(runs):
             if 0 < r <= len(runs) - RAW_BUFS:
                 load_run(r + RAW_BUFS - 1)
-            may_scale = r >= SCALE_FROM
-            may_store = r >= len(runs) - RAW_BUFS
-            ahead = runs[r + 1] if r + 1 < len(runs) else []
-            sorts = {"": [], "vector": [], "scalar": []}
-            for j, piece in enumerate(ahead):
-                engine = (SORTER, SORTER2)[j][r + 1]
-                sorts[engine].extend([(piece, engine, a) for a in range(2)])
+            busy = r >= FIRST_BUSY_RUN
+            sorts = {"vector": [], "scalar": []}
+            for j, piece in enumerate(runs[r + 1] if r + 1 < len(runs) else []):
+                if sorter(r + 1, j):
+                    sorts[sorter(r + 1, j)].extend([(piece, sorter(r + 1, j), a) for a in range(2)])
+
             grouped = []
             for j, piece in enumerate(run):
                 grouped.append(stage.tile([P, 4 * BANK], BF16, name="grouped", align_bytes=64))
-                if r == 0:
-                    for b in BIAS_AT[j]:
-                        spread_bias(b)
                 for a in range(2):
-                    transpose_half(piece, grouped[j], a)
-                combine(may_scale, may_store)
+                    transpose_bank(piece, grouped[j], a)
+                if busy:
+                    shift_step()
                 if j == 0:
                     quantize(piece, grouped[j])
+                empty_banks()
             for job in sorts["vector"]:
                 sort_words(*job)
-            early = r < Q_LATE_FROM
-            if early:
+            second_waits = busy
+            if not second_waits:
                 quantize(run[1], grouped[1])
             exponentiate()
-            for i, (unit, t, g) in enumerate(matmuls[r]):
+
+            for i, (unit, t, g) in enumerate(passes_after[r]):
                 if (t, g) == (0, 0):
-                    if sorts["scalar"]:
-                        sort_words(*sorts["scalar"].pop(0))
-                        if i == 0 and FIRST2 and sorts["scalar"]:
-                            sort_words(*sorts["scalar"].pop(0))
+                    for job in sorts["scalar"][: 2 if i == 0 else 1]:
+                        sort_words(*job)
+                        sorts["scalar"].remove(job)
                     exponentiate()
                 multiply(unit, t, g)
                 if (t, g) == (unit[1] - 1, PASSES - 1):
-                    add_bias(unit)
-                    if not early:
+                    closed.append(unit)
+                    empty_banks()
+                    if second_waits:
                         quantize(run[1], grouped[1])
-                        early = True
-                    combine(may_scale, may_store)
+                        second_waits = False
+                    if busy:
+                        shift_step()
+                    empty_banks()
+                    if r >= len(runs) - RAW_BUFS:
+                        store()
             for job in sorts["scalar"]:
                 sort_words(*job)
-        exponentiate()
-        for i in range(4):
-            combine(True, True)
+        assert not (closed or summed or exped or scaled or finished)

@@ -70,6 +70,7 @@ def tile_vae_pb_kernel(tc, hd, W_mu_d, b_mu_d, W_ls_d, b_ls_d, eps_x, out):
 
     passes = [(unit, t, g) for unit in units for t in range(unit[1]) for g in range(PASSES)]
     ends = [0, PASSES // 2] + [2 * PASSES * ready[r - 1] for r in range(2, len(runs) - 1)] + [len(passes)]
+    ends[-2] = ends[-2] + 2 * PASSES
     passes_after = [passes[start:end] for start, end in zip([0] + ends, ends)]
 
     eps_after = {runs.index([("h", 2 * i, 0), ("h", 2 * i + 1, 0)]): (i, i + 1, 0) for i in range(1, PAIRS)}
@@ -93,40 +94,32 @@ def tile_vae_pb_kernel(tc, hd, W_mu_d, b_mu_d, W_ls_d, b_ls_d, eps_x, out):
             nc.sync.dma_start(out=folded[j * P // 2 : (j + 1) * P // 2, :], in_=vec.rearrange("(p e) -> p e", e=FOLD))
         bias = keep.tile([P, 2, XO], F32, name="bias")
 
-        def spread_biases():
+        def spread_biases(first, copy):
             per_bank = BANK // P
-            for e0 in range(0, FOLD, per_bank):
+            for e0 in range(first, first + FOLD // 2, per_bank):
                 spread = psum.tile([P, per_bank, P], F32, name="acc")
                 for i in range(per_bank):
                     column = folded[:, e0 + i : e0 + i + 1].to_broadcast([P, P])
                     nc.tensor.matmul(out=spread[:, i, :], lhsT=column, rhs=ident_bf[:], start=True, stop=True)
                 dst = bias[:].rearrange("p j (n e) -> p (j n) e", e=FOLD)[:, :, e0 : e0 + per_bank]
-                nc.vector.tensor_copy(out=dst, in_=spread[:].rearrange("p e n -> p n e"))
+                copy(out=dst, in_=spread[:].rearrange("p e n -> p n e"))
 
         eps = [keep.tile([P, B // P, XO // 2], BF16, name="eps_%d" % half) for half in range(2)]
         words = {}
 
         def load_run(r):
             raw = stage.tile([P, 2, K], BF16, name="raw", bufs=RAW_BUFS)
-            (kind0, i0, half0), (kind1, i1, half1) = runs[r]
-            view = raw[:].bitcast(F32)
-            if kind0 == "h":
-                nc.sync.dma_start(out=raw[:], in_=hd[i0 * P : (i0 + 2) * P, :].rearrange("(t p) k -> p t k", p=P))
-                for j, piece in enumerate(runs[r]):
-                    words[piece] = view[:, j, :].rearrange("p (a b w) -> p a b w", a=2, b=2)
-            else:
-                matrix, q = strips[i0]
-                rows = (W_mu_d, W_ls_d)[matrix][q * COLS : (q + 1) * COLS, :].rearrange("(b p) k -> p b k", p=P)
-                if kind1 == "w":
-                    nc.sync.dma_start(out=raw[:], in_=rows)
-                    for j, piece in enumerate(runs[r]):
-                        words[piece] = view[:, :, j * BANK : (j + 1) * BANK].rearrange("p b (a w) -> p a b w", a=2)
+            for j, piece in enumerate(runs[r]):
+                operand, i, half = piece
+                view = raw[:].bitcast(F32)[:, j, :]
+                if operand == "h":
+                    nc.sync.dma_start(out=raw[:, j, :], in_=hd[i * P : (i + 1) * P, :])
+                    words[piece] = view.rearrange("p (a b w) -> p a b w", a=2, b=2)
                 else:
-                    ks = slice(half0 * K // 2, (half0 + 1) * K // 2)
-                    nc.sync.dma_start(out=raw[:, 0, :].rearrange("p (b k) -> p b k", b=2), in_=rows[:, :, ks])
-                    nc.sync.dma_start(out=raw[:, 1, :], in_=hd[i1 * P : (i1 + 1) * P, :])
-                    words[runs[r][0]] = view[:, 0, :].rearrange("p (b a w) -> p a b w", a=2, b=2)
-                    words[runs[r][1]] = view[:, 1, :].rearrange("p (a b w) -> p a b w", a=2, b=2)
+                    matrix, q = strips[i]
+                    rows = (W_mu_d, W_ls_d)[matrix][q * COLS : (q + 1) * COLS, half * K // 2 : (half + 1) * K // 2]
+                    nc.sync.dma_start(out=raw[:, j, :].rearrange("p (b k) -> p b k", b=2), in_=rows.rearrange("(b p) k -> p b k", p=P))
+                    words[piece] = view.rearrange("p (b a w) -> p a b w", a=2, b=2)
             if r in eps_after:
                 first, end, half = eps_after[r]
                 rows = eps_x[2 * first * P : 2 * end * P, half * XO // 2 : (half + 1) * XO // 2]
@@ -233,7 +226,7 @@ def tile_vae_pb_kernel(tc, hd, W_mu_d, b_mu_d, W_ls_d, b_ls_d, eps_x, out):
 
         for r in range(RAW_BUFS):
             load_run(r)
-        spread_biases()
+        spread_biases(0, nc.vector.tensor_copy)
         for r, run in enumerate(runs):
             if 0 < r <= len(runs) - RAW_BUFS:
                 load_run(r + RAW_BUFS - 1)
@@ -253,6 +246,8 @@ def tile_vae_pb_kernel(tc, hd, W_mu_d, b_mu_d, W_ls_d, b_ls_d, eps_x, out):
                 if j == 0:
                     quantize(piece, grouped[j])
                 empty_banks()
+            if r == 1:
+                spread_biases(FOLD // 2, nc.scalar.copy)
             for job in sorts["vector"]:
                 sort_words(*job)
             second_waits = busy

from contextlib import ExitStack

import concourse.mybir as mybir
from concourse.masks import make_identity

B, K, XO = 1024, 2048, 1024
FLOPS = 2 * 2 * B * K * XO

F32 = mybir.dt.float32
BF16 = mybir.dt.bfloat16
U32 = mybir.dt.uint32
U8 = mybir.dt.uint8
E5M2X4 = mybir.dt.float8_e5m2_x4
E4M3X4 = mybir.dt.float8_e4m3fn_x4
ADD = mybir.AluOpType.add
MULT = mybir.AluOpType.mult
EXP = mybir.ActivationFunctionType.Exp

P = 128
PASSES = K // 512
WORDS = 256
BANK = 512
COLS = 256
PAIRS = B // (2 * P)
FOLD = 2 * XO // P
MU, LS = 0, 1

FIRST_SORTED_RUN = 2
FIRST_SCALAR_RUN = 5
FIRST_FULL_SCALAR_RUN = 7
FIRST_BUSY_RUN = 4

RAW_BUFS = 6
RESULT_BUFS = 8
SHIFTED_BUFS = 12
LS_BUFS = 4


def sorter(r, j):
    if r < FIRST_SORTED_RUN or (j == 0 and FIRST_SCALAR_RUN <= r < FIRST_FULL_SCALAR_RUN):
        return None
    return "vector" if r < FIRST_SCALAR_RUN else "scalar"


def tile_vae_pb_kernel(tc, hd, W_mu_d, b_mu_d, W_ls_d, b_ls_d, eps_x, out):
    nc = tc.nc

    quarters = XO // COLS
    strips = [(LS, 0)]
    for q in range(quarters - 1):
        strips.extend([(LS, q + 1), (MU, q)])
    strips.append((MU, quarters - 1))

    runs = [[("w", 0, 0), ("h", 0, 0)], [("w", 0, 1), ("h", 1, 0)]]
    units = [(0, 2, 0)]
    ready = [0, 1]
    for i in range(1, PAIRS):
        runs.append([("w", i, 0), ("w", i, 1)])
        units.extend([(2 * pair, 2, i) for pair in range(i)])
        ready.append(len(units))
        runs.append([("h", 2 * i, 0), ("h", 2 * i + 1, 0)])
        units.extend([(2 * i, 2, s) for s in sorted(range(i + 1), key=lambda s: strips[s][0] == MU)])
        ready.append(len(units))
    for s in range(PAIRS, len(strips)):
        runs.append([("w", s, 0), ("w", s, 1)])
        units.extend([(2 * pair, 2, s) for pair in range(PAIRS)])
        ready.append(len(units))
    m_last, count_last, s_last = units.pop()
    units.extend([(m_last + t, 1, s_last) for t in range(count_last)])

    passes = [(unit, t, g) for unit in units for t in range(unit[1]) for g in range(PASSES)]
    ends = [0, PASSES // 2] + [2 * PASSES * ready[r - 1] for r in range(2, len(runs) - 1)] + [len(passes)]
    ends[-2] = ends[-2] + 2 * PASSES
    passes_after = [passes[start:end] for start, end in zip([0] + ends, ends)]

    eps_after = {runs.index([("h", 2 * i, 0), ("h", 2 * i + 1, 0)]): (i, i + 1, 0) for i in range(1, PAIRS)}
    eps_after[min(eps_after)] = (0, 2, 0)
    first_right = strips.index((LS, quarters // 2))
    eps_after[runs.index([("w", first_right, 0), ("w", first_right, 1)])] = (0, PAIRS, 1)

    with ExitStack() as ctx:
        keep = ctx.enter_context(tc.tile_pool(name="keep", bufs=1))
        stage = ctx.enter_context(tc.tile_pool(name="stage", bufs=4))
        psum = ctx.enter_context(tc.psum_pool(name="psum", bufs=4))
        ctx.enter_context(tc.manual_schedule())

        ident = keep.tile([P, P], F32, name="ident")
        make_identity(nc, ident[:])
        ident_bf = keep.tile([P, P], BF16, name="ident_bf")
        nc.vector.tensor_copy(out=ident_bf[:], in_=ident[:])

        folded = keep.tile([P, FOLD], BF16, name="folded")
        for j, vec in enumerate((b_mu_d, b_ls_d)):
            nc.sync.dma_start(out=folded[j * P // 2 : (j + 1) * P // 2, :], in_=vec.rearrange("(p e) -> p e", e=FOLD))
        bias = keep.tile([P, 2, XO], F32, name="bias")

        def spread_biases(first, copy):
            per_bank = BANK // P
            for e0 in range(first, first + FOLD // 2, per_bank):
                spread = psum.tile([P, per_bank, P], F32, name="acc")
                for i in range(per_bank):
                    column = folded[:, e0 + i : e0 + i + 1].to_broadcast([P, P])
                    nc.tensor.matmul(out=spread[:, i, :], lhsT=column, rhs=ident_bf[:], start=True, stop=True)
                dst = bias[:].rearrange("p j (n e) -> p (j n) e", e=FOLD)[:, :, e0 : e0 + per_bank]
                copy(out=dst, in_=spread[:].rearrange("p e n -> p n e"))

        eps = [keep.tile([P, B // P, XO // 2], BF16, name="eps_%d" % half) for half in range(2)]
        words = {}

        def load_run(r):
            raw = stage.tile([P, 2, K], BF16, name="raw", bufs=RAW_BUFS)
            for j, piece in enumerate(runs[r]):
                operand, i, half = piece
                view = raw[:].bitcast(F32)[:, j, :]
                if operand == "h":
                    nc.sync.dma_start(out=raw[:, j, :], in_=hd[i * P : (i + 1) * P, :])
                    words[piece] = view.rearrange("p (a b w) -> p a b w", a=2, b=2)
                else:
                    matrix, q = strips[i]
                    rows = (W_mu_d, W_ls_d)[matrix][q * COLS : (q + 1) * COLS, half * K // 2 : (half + 1) * K // 2]
                    nc.sync.dma_start(out=raw[:, j, :].rearrange("p (b k) -> p b k", b=2), in_=rows.rearrange("(b p) k -> p b k", p=P))
                    words[piece] = view.rearrange("p (b a w) -> p a b w", a=2, b=2)
            if r in eps_after:
                first, end, half = eps_after[r]
                rows = eps_x[2 * first * P : 2 * end * P, half * XO // 2 : (half + 1) * XO // 2]
                nc.sync.dma_start(out=eps[half][:, 2 * first : 2 * end, :], in_=rows.rearrange("(t p) x -> p t x", p=P))

        sorted_words = {}
        codes, scales = {}, {}
        acc = {}
        shifted = {}
        closed, summed, exped, scaled, finished = [], [], [], [], []

        def sort_words(piece, engine, a):
            if a == 0:
                sorted_words[piece] = stage.tile([P, 2, 2, 2, P], F32, name="sorted")
            src = words[piece][:, a, :, :].rearrange("p b (w u) -> p b u w", u=2)
            if engine == "vector":
                nc.vector.tensor_copy(out=sorted_words[piece][:, a, :, :, :], in_=src)
            else:
                nc.scalar.copy(out=sorted_words[piece][:, a, :, :, :], in_=src)

        def transpose_bank(piece, grouped, a):
            bank = psum.tile([P, 2, 2, P], F32, name="xt")
            for b in range(2):
                for u in range(2):
                    if piece in sorted_words:
                        src = sorted_words[piece][:, a, b, u, :]
                    else:
                        src = words[piece][:, a, b, u:WORDS:2]
                    nc.tensor.transpose(bank[:, b, u, :], src, ident[:])
            dst = grouped[:].bitcast(F32)[:, a * BANK : (a + 1) * BANK]
            nc.scalar.copy(out=dst.rearrange("p (b c u) -> p b c u", b=2, u=2), in_=bank[:].rearrange("p b u c -> p b c u"))

        def quantize(piece, grouped):
            codes[piece] = keep.tile([P, BANK], U32, name="codes_%s_%d_%d" % piece, align_bytes=64)
            scales[piece] = keep.tile([P, BANK], U8, name="scales_%s_%d_%d" % piece, align_bytes=64)
            fmt = E5M2X4 if piece[0] == "h" else E4M3X4
            nc.vector.quantize_mx(out=codes[piece][:].bitcast(fmt), scales=scales[piece][:], in_=grouped[:])

        def multiply(unit, t, g):
            m, count, s = unit
            if (t, g) == (0, 0):
                acc[unit] = psum.tile([P, count, COLS], F32, name="acc")
            h_piece, w_piece = ("h", m + t, 0), ("w", s, g // 2)
            h_cols = slice(g * P, (g + 1) * P)
            w_cols = slice((g % 2) * COLS, (g % 2 + 1) * COLS)
            nc.tensor.matmul_mx(
                out=acc[unit][:, t, :],
                lhsT=codes[h_piece][:, h_cols].bitcast(E5M2X4),
                lhsT_scale=scales[h_piece][:, h_cols],
                rhs=codes[w_piece][:, w_cols].bitcast(E4M3X4),
                rhs_scale=scales[w_piece][:, w_cols],
                start=(g == 0),
                stop=(g == PASSES - 1),
            )

        def bias_of(matrix, unit):
            m, count, s = unit
            q = strips[s][1]
            return bias[:, matrix, q * COLS : (q + 1) * COLS].unsqueeze(1).to_broadcast([P, count, COLS])

        def empty_banks():
            for unit in list(closed):
                m, count, s = unit
                matrix, q = strips[s]
                t = m % 2
                if matrix == LS:
                    ls = stage.tile([P, count, COLS], F32, name="ls", bufs=LS_BUFS)
                    nc.vector.tensor_tensor(out=ls[:], in0=acc[unit][:], in1=bias_of(LS, unit), op=ADD)
                    summed.append((unit, ls))
                    closed.remove(unit)
                elif (m - t, q) in shifted:
                    result = stage.tile([P, count, COLS], F32, name="result", bufs=RESULT_BUFS)
                    nc.vector.tensor_tensor(out=result[:], in0=acc[unit][:], in1=shifted[(m - t, q)][:, t : t + count, :], op=ADD)
                    finished.append((unit, result))
                    closed.remove(unit)

        def exponentiate():
            for unit, ls in summed:
                std = stage.tile([P, 2, COLS], F32, name="std", bufs=LS_BUFS)
                nc.scalar.activation(out=std[:], in_=ls[:], func=EXP, scale=0.5)
                exped.append((unit, std))
            summed.clear()

        def shift_step():
            if scaled:
                unit, noise = scaled.pop(0)
                key = (unit[0], strips[unit[2]][1])
                shifted[key] = stage.tile([P, 2, COLS], F32, name="shifted", bufs=SHIFTED_BUFS)
                nc.vector.tensor_tensor(out=shifted[key][:], in0=noise[:], in1=bias_of(MU, unit), op=ADD)
            elif exped:
                unit, std = exped.pop(0)
                m, count, s = unit
                noise = stage.tile([P, 2, COLS], F32, name="noise", bufs=2)
                half, c = divmod(strips[s][1] * COLS, XO // 2)
                nc.vector.tensor_tensor(out=noise[:], in0=std[:], in1=eps[half][:, m : m + 2, c : c + COLS], op=MULT)
                scaled.append((unit, noise))

        def store():
            for (m, count, s), result in finished:
                q = strips[s][1]
                rows = out[m * P : (m + count) * P, q * COLS : (q + 1) * COLS]
                nc.sync.dma_start(out=rows.rearrange("(t p) x -> p t x", p=P), in_=result[:])
            finished.clear()

        for r in range(RAW_BUFS):
            load_run(r)
        spread_biases(0, nc.vector.tensor_copy)
        for r, run in enumerate(runs):
            if 0 < r <= len(runs) - RAW_BUFS:
                load_run(r + RAW_BUFS - 1)
            busy = r >= FIRST_BUSY_RUN
            sorts = {"vector": [], "scalar": []}
            for j, piece in enumerate(runs[r + 1] if r + 1 < len(runs) else []):
                if sorter(r + 1, j):
                    sorts[sorter(r + 1, j)].extend([(piece, sorter(r + 1, j), a) for a in range(2)])

            grouped = []
            for j, piece in enumerate(run):
                grouped.append(stage.tile([P, 4 * BANK], BF16, name="grouped", align_bytes=64))
                for a in range(2):
                    transpose_bank(piece, grouped[j], a)
                if busy:
                    shift_step()
                if j == 0:
                    quantize(piece, grouped[j])
                empty_banks()
            if r == 1:
                spread_biases(FOLD // 2, nc.scalar.copy)
            for job in sorts["vector"]:
                sort_words(*job)
            second_waits = busy
            if not second_waits:
                quantize(run[1], grouped[1])
            exponentiate()

            for i, (unit, t, g) in enumerate(passes_after[r]):
                if (t, g) == (0, 0):
                    for job in sorts["scalar"][: 2 if i == 0 else 1]:
                        sort_words(*job)
                        sorts["scalar"].remove(job)
                    exponentiate()
                multiply(unit, t, g)
                if (t, g) == (unit[1] - 1, PASSES - 1):
                    closed.append(unit)
                    empty_banks()
                    if second_waits:
                        quantize(run[1], grouped[1])
                        second_waits = False
                    if busy:
                        shift_step()
                    empty_banks()
                    if r >= len(runs) - RAW_BUFS:
                        store()
            for job in sorts["scalar"]:
                sort_words(*job)
        assert not (closed or summed or exped or scaled or finished)
